import numpy as np
import ml_dtypes


def mxq(x, axis, fmt="e4m3"):
    dtype, down = {"e4m3": (ml_dtypes.float8_e4m3fn, 7), "e5m2": (ml_dtypes.float8_e5m2, 14)}[fmt]
    v = np.moveaxis(np.asarray(x, np.float32).astype(ml_dtypes.bfloat16).astype(np.float64), axis, -1)
    blocks = v.reshape(v.shape[:-1] + (-1, 32))
    amax = np.abs(blocks).max(-1, keepdims=True)
    byte = np.maximum(np.where(amax > 0, np.frexp(amax)[1] - 1 + 127, 0) - down, 1)
    scale = np.exp2(byte - 127.0)
    codes = (blocks / scale).astype(np.float32).astype(dtype).astype(np.float64)
    return np.moveaxis((codes * scale).reshape(v.shape), -1, axis)


WIDE = False


def mx_kscale(k):
    if not WIDE:
        return np.ones(k)
    levels = np.array([10, -10, 5, -5, 0])
    if k % 512:
        return np.exp2(np.random.permutation(np.resize(levels, k // 32))).repeat(32)
    a = np.empty((k // 512, 16))
    for p in range(k // 512):
        a[p, :8] = np.random.permutation(np.resize(levels, 8))
        for g in range(8):
            far = levels[np.abs(levels - a[p, g]) >= 10]
            a[p, g + 8] = far[np.random.randint(len(far))]
    return np.exp2(a.ravel()).repeat(32)


BF16 = ml_dtypes.bfloat16


def bf(x):
    return np.asarray(x, np.float32).astype(BF16)


def f64(x):
    return np.asarray(x).astype(np.float64)


B, CK, CV, NO, T, H, W = 1, 128, 512, 3, 4, 32, 16
N = T * H * W
P = H * W
C = NO * CV


def setup_inputs():
    s = mx_kscale(N)
    g = np.exp2(np.round(np.log2(np.mean(s))))
    mk = np.random.standard_normal((B, CK, N))
    qk = np.random.standard_normal((B, CK, P))
    qe = np.random.uniform(0.0, 1.0, (B, CK, P))
    ms = bf(0.75 + 0.5 * np.random.uniform(0.0, 1.0, (B, N)))
    d = (np.log2(np.max(s)) - np.log2(s))[None, :] * np.log(2.0) * np.sqrt(CK) / f64(ms)
    a0 = mk[:, 0, :] ** 2 + d
    mk[:, 0, :] = np.sqrt(a0)
    qk[:, 0, :] = 0.0
    qe[:, 0, :] = 1.0
    mk, qk, qe = bf(mk), bf(qk), bf(qe)
    mksq = f64(mk) * f64(mk)
    mksq[:, 0, :] = a0
    return {"memory_key": mk,
            "memory_key_sq": bf(mksq),
            "query_key": qk,
            "query_selection": qe,
            "query_key_sel": bf(f64(qk) * f64(qe)),
            "memory_shrinkage": ms,
            "memory_value": bf(np.random.standard_normal((B, C, N)) * g / s[None, None, :])}


def reference(memory_key, memory_key_sq, query_key, query_selection, query_key_sel, memory_shrinkage, memory_value):
    qe = f64(query_selection)
    qs = f64(query_key_sel)
    ms = f64(memory_shrinkage)[:, :, None]
    a_sq = f64(memory_key_sq).transpose(0, 2, 1) @ qe
    two_ab = 2.0 * (f64(memory_key).transpose(0, 2, 1) @ qs)
    b_sq = np.sum(qs * f64(query_key), axis=1, keepdims=True)
    similarity = (-a_sq + two_ab - b_sq) * ms * (1.0 / np.sqrt(CK))
    e = np.exp(similarity - similarity.max(axis=1, keepdims=True))
    affinity = e / e.sum(axis=1, keepdims=True)
    return mxq(f64(memory_value), 2, "e4m3") @ mxq(affinity, 1, "e4m3")

@@ -1,0 +1,322 @@
+import math
+from contextlib import ExitStack
+
+import concourse.mybir as mybir
+from concourse.masks import make_identity
+
+F32 = mybir.dt.float32
+BF16 = mybir.dt.bfloat16
+U32 = mybir.dt.uint32
+U8 = mybir.dt.uint8
+FP8X4 = mybir.dt.float8_e4m3fn_x4
+ALU = mybir.AluOpType
+ACT = mybir.ActivationFunctionType
+AXIS = mybir.AxisListType
+
+P = 128
+KEY_CHANNELS = 128
+MEMORY = 2048
+QUERIES = 512
+VALUE_CHANNELS = 1536
+PACK = 4
+K_PASS = P * PACK
+PASSES = MEMORY // K_PASS
+HALF = MEMORY // 2
+QUERY_TILES = QUERIES // P
+VALUE_TILES = VALUE_CHANNELS // P
+BANK = 512
+TILES_PER_BANK = BANK // P
+VALUE_BANKS = VALUE_TILES // TILES_PER_BANK
+ROUNDS = QUERY_TILES + 2
+
+INV_SQRT_CK = 1.0 / math.sqrt(KEY_CHANNELS)
+
+FLOPS = 2 * VALUE_CHANNELS * MEMORY * QUERIES + 2 * 2 * KEY_CHANNELS * MEMORY * QUERIES
+
+
+def pass_order(columns):
+    return columns.rearrange("c (q t) -> c t q", t=PACK)
+
+
+def tile_vidsam_pa_kernel(
+    tc,
+    memory_key,
+    memory_key_sq,
+    query_key,
+    query_selection,
+    query_key_sel,
+    memory_shrinkage,
+    memory_value,
+    out,
+):
+    nc = tc.nc
+    with ExitStack() as stack:
+        const = stack.enter_context(tc.tile_pool(name="const", bufs=1))
+        raw_pool = stack.enter_context(tc.tile_pool(name="raw", bufs=VALUE_TILES))
+        work = stack.enter_context(tc.tile_pool(name="work", bufs=2))
+        small = stack.enter_context(tc.tile_pool(name="small", bufs=4))
+        stage = stack.enter_context(tc.tile_pool(name="stage", bufs=4))
+        psum_sim = stack.enter_context(tc.psum_pool(name="psum_sim", bufs=2))
+        psum_tr = stack.enter_context(tc.psum_pool(name="psum_tr", bufs=4))
+        psum_acc = stack.enter_context(tc.psum_pool(name="psum_acc", bufs=2))
+        stack.enter_context(tc.manual_schedule())
+
+        shrink_in = const.tile([1, MEMORY], BF16)
+        nc.sync.dma_start(out=shrink_in[:], in_=memory_shrinkage)
+        qs = const.tile([P, QUERIES], BF16)
+        nc.sync.dma_start(out=qs[:], in_=query_key_sel.flatten_outer_dims())
+        qk = const.tile([P, QUERIES], BF16)
+        nc.sync.dma_start(out=qk[:], in_=query_key.flatten_outer_dims())
+        qe = const.tile([P, QUERIES], BF16)
+        nc.sync.dma_start(out=qe[:], in_=query_selection.flatten_outer_dims())
+        mksq = const.tile([P, MEMORY], BF16)
+        mk = const.tile([P, MEMORY], BF16)
+        values = memory_value.flatten_outer_dims()
+        raw_tiles = []
+
+        def load_keys(h):
+            cols = slice(h * HALF, (h + 1) * HALF)
+            nc.sync.dma_start(out=mksq[:, cols], in_=memory_key_sq.flatten_outer_dims()[:, cols])
+            nc.sync.dma_start(out=mk[:, cols], in_=memory_key.flatten_outer_dims()[:, cols])
+
+        def load_values(m):
+            raw = raw_pool.tile([P, MEMORY], BF16, name="raw")
+            nc.sync.dma_start(out=raw[:], in_=values[m * P : (m + 1) * P, :])
+            raw_tiles.append(raw)
+
+        load_keys(0)
+        load_values(0)
+        load_keys(1)
+        for m in range(1, VALUE_TILES):
+            load_values(m)
+
+        shrink_row = const.tile([P, MEMORY], BF16)
+        nc.gpsimd.memset(shrink_row[:].bitcast(F32), 0.0)
+        ones_bf16 = const.tile([P, P], BF16)
+        nc.vector.memset(ones_bf16[:], 1.0)
+        ones_f32 = const.tile([P, 2], F32)
+        nc.vector.memset(ones_f32[:], 1.0)
+        zero_col = const.tile([P, 1], F32)
+        nc.vector.memset(zero_col[:], 0.0)
+        one_col = const.tile([P, 1], F32)
+        nc.scalar.activation(out=one_col[:], in_=zero_col[:], func=ACT.Exp)
+        nc.vector.tensor_copy(out=shrink_row[0:1, :], in_=shrink_in[:])
+        ident_f32 = const.tile([P, P], F32)
+        make_identity(nc, ident_f32[:])
+        ident_bf16 = const.tile([P, P], BF16)
+        make_identity(nc, ident_bf16[:])
+
+        qs_m2 = const.tile([P, QUERIES], BF16)
+        nc.vector.tensor_scalar(out=qs_m2[:], in0=qs[:], scalar1=-2.0, scalar2=None, op0=ALU.mult)
+        qs_qk = const.tile([P, QUERIES], F32)
+        nc.vector.tensor_tensor(out=qs_qk[:, 0:P], in0=qs[:, 0:P], in1=qk[:, 0:P], op=ALU.mult)
+        nc.vector.tensor_tensor(out=qs_qk[:, P:], in0=qs[:, P:], in1=qk[:, P:], op=ALU.mult)
+        b_sq = const.tile([P, QUERY_TILES], F32)
+        factor = const.tile([P, MEMORY], F32)
+
+        value_codes = const.tile([P, VALUE_TILES, PASSES, P], U32, align_bytes=64)
+        value_scales = const.tile([P, VALUE_TILES, PASSES, P], U8, align_bytes=64)
+        aff_codes = const.tile([P, QUERY_TILES, PASSES, P], U32, align_bytes=64)
+        aff_scales = const.tile([P, QUERY_TILES, PASSES, P], U8, align_bytes=64)
+        out_view = out.flatten_outer_dims().rearrange("(m c) p -> c m p", c=P)
+
+        scaled = {}
+        shift = {}
+        expo = {}
+        total = {}
+        inverse = {}
+        aff = {}
+        aff_grouped = {}
+        value_grouped = {}
+
+        def query_norms(first, last):
+            b_sq_bank = psum_acc.tile([P, QUERY_TILES, 2], F32, tag="acc")
+            for i in range(first, last):
+                nc.tensor.matmul(
+                    out=b_sq_bank[:, i, :],
+                    lhsT=qs_qk[:, i * P : (i + 1) * P],
+                    rhs=ones_f32[:],
+                    start=True,
+                    stop=True,
+                )
+            nc.vector.tensor_copy(out=b_sq[:, first:last], in_=b_sq_bank[:, first:last, 0])
+
+        def spread_shrinkage(g):
+            cols = slice(g * K_PASS, (g + 1) * K_PASS)
+            spread = psum_tr.tile([P, PACK, P], F32, tag="turned")
+            nc.tensor.matmul(
+                out=spread[:], lhsT=ones_bf16[:], rhs=pass_order(shrink_row[:, cols]), start=True, stop=True
+            )
+            nc.scalar.mul(out=factor[:, cols], in_=spread[:].rearrange("p t q -> p (t q)"), mul=-INV_SQRT_CK)
+
+        def distances(i, g):
+            if not 0 <= i < QUERY_TILES:
+                return
+            if g == 0:
+                scaled[i] = work.tile([P, MEMORY], F32, name="scaled")
+            cols = slice(g * K_PASS, (g + 1) * K_PASS)
+            dist = psum_sim.tile([P, PACK, P], F32, tag="sim")
+            nc.tensor.matmul(
+                out=dist[:], lhsT=qe[:, i * P : (i + 1) * P], rhs=pass_order(mksq[:, cols]), start=True, stop=False
+            )
+            nc.tensor.matmul(
+                out=dist[:], lhsT=qs_m2[:, i * P : (i + 1) * P], rhs=pass_order(mk[:, cols]), start=False, stop=True
+            )
+            nc.vector.scalar_tensor_tensor(
+                out=scaled[i][:, cols],
+                in0=dist[:].rearrange("p t q -> p (t q)"),
+                scalar=b_sq[:, i : i + 1],
+                in1=factor[:, cols],
+                op0=ALU.add,
+                op1=ALU.mult,
+            )
+
+        def maximum(i):
+            if not 0 <= i < QUERY_TILES:
+                return
+            shift[i] = small.tile([P, 1], F32, name="shift")
+            nc.vector.tensor_reduce(out=shift[i][:], in_=scaled[i][:], axis=AXIS.X, op=ALU.max, negate=True)
+
+        def exponentials(i):
+            if not 0 <= i < QUERY_TILES:
+                return
+            expo[i] = work.tile([P, MEMORY], F32, name="expo")
+            total[i] = small.tile([P, 1], F32, name="total")
+            nc.scalar.activation(
+                out=expo[i][:],
+                in_=scaled[i][:],
+                func=ACT.Exp,
+                bias=shift[i][:],
+                accum_out=total[i][:],
+            )
+
+        def invert_total(i):
+            if not 0 <= i < QUERY_TILES:
+                return
+            inverse[i] = small.tile([P, 1], F32, name="inverse")
+            nc.vector.reciprocal(out=inverse[i][:], in_=total[i][:])
+
+        def normalise(i, half):
+            if not 0 <= i < QUERY_TILES:
+                return
+            if half == 0:
+                aff[i] = work.tile([P, MEMORY], BF16, name="aff")
+            cols = slice(half * HALF, (half + 1) * HALF)
+            nc.vector.tensor_scalar(
+                out=aff[i][:, cols], in0=expo[i][:, cols], scalar1=inverse[i][:], scalar2=None, op0=ALU.mult
+            )
+
+        def turn_affinity(i, half):
+            if not 0 <= i < QUERY_TILES:
+                return
+            if half == 0:
+                aff_grouped[i] = work.tile([P, PASSES, P, PACK], BF16, name="aff_grouped", align_bytes=64)
+            turned = psum_tr.tile([P, 2, PACK, P], BF16, tag="turned")
+            for gl in range(2):
+                for t in range(PACK):
+                    first = (2 * half + gl) * K_PASS + t * P
+                    nc.tensor.transpose(turned[:, gl, t, :], aff[i][:, first : first + P], ident_bf16[:])
+            nc.scalar.copy(
+                out=aff_grouped[i][:, 2 * half : 2 * half + 2, :, :],
+                in_=turned[:].rearrange("q g t p -> q g p t"),
+            )
+
+        def quantise_affinity(i, half):
+            if not 0 <= i < QUERY_TILES:
+                return
+            two = slice(2 * half, 2 * half + 2)
+            nc.vector.quantize_mx(
+                out=aff_codes[:, i, two, :].rearrange("q g p -> q (g p)").bitcast(FP8X4),
+                scales=aff_scales[:, i, two, :].rearrange("q g p -> q (g p)"),
+                in_=aff_grouped[i][:, two, :, :].rearrange("q g p t -> q (g p t)"),
+            )
+
+        def turn_values(m):
+            if not 0 <= m < VALUE_TILES:
+                return
+            words = raw_tiles[m][:].bitcast(F32)
+            value_grouped[m] = stage.tile([P, PASSES, P, 2], F32, name="value_grouped", align_bytes=64)
+            for half in range(2):
+                turned = psum_tr.tile([P, 2, 2, P], F32, tag="turned")
+                for gl in range(2):
+                    for u in range(2):
+                        first = (2 * half + gl) * 2 * P + u
+                        nc.tensor.transpose(
+                            turned[:, gl, u, :], words[:, first : first + 2 * P - 1 : 2], ident_f32[:]
+                        )
+                nc.scalar.copy(
+                    out=value_grouped[m][:, 2 * half : 2 * half + 2, :, :],
+                    in_=turned[:].rearrange("q g u c -> q g c u"),
+                )
+
+        def quantise_values(m):
+            if not 0 <= m < VALUE_TILES:
+                return
+            nc.vector.quantize_mx(
+                out=value_codes[:, m, :, :].rearrange("q g c -> q (g c)").bitcast(FP8X4),
+                scales=value_scales[:, m, :, :].rearrange("q g c -> q (g c)"),
+                in_=value_grouped[m][:].rearrange("q g c u -> q (g c u)").bitcast(BF16),
+            )
+
+        def product(i, b, copy_engine):
+            acc = psum_acc.tile([P, TILES_PER_BANK, P], F32, tag="acc")
+            for cell in range(TILES_PER_BANK):
+                m = b * TILES_PER_BANK + cell
+                for g in range(PASSES):
+                    nc.tensor.matmul_mx(
+                        out=acc[:, cell, :],
+                        lhsT=value_codes[:, m, g, :].bitcast(FP8X4),
+                        lhsT_scale=value_scales[:, m, g, :],
+                        rhs=aff_codes[:, i, g, :].bitcast(FP8X4),
+                        rhs_scale=aff_scales[:, i, g, :],
+                        start=(g == 0),
+                        stop=(g == PASSES - 1),
+                    )
+            result = stage.tile([P, TILES_PER_BANK, P], F32, name="result")
+            if copy_engine == "vector":
+                nc.vector.tensor_copy(out=result[:], in_=acc[:])
+            else:
+                nc.scalar.copy(out=result[:], in_=acc[:])
+            nc.sync.dma_start(
+                out=out_view[:, b * TILES_PER_BANK : (b + 1) * TILES_PER_BANK, i * P : (i + 1) * P],
+                in_=result[:],
+            )
+
+        def products(r, k):
+            due = sorted((b, i) for i in range(QUERY_TILES) for b in range(VALUE_BANKS) if max(i + 2, b + 1) == r)
+            if k < len(due):
+                b, i = due[k]
+                product(i, b, "scalar" if k == 0 else "vector")
+
+        for g in range(PASSES):
+            spread_shrinkage(g)
+        query_norms(0, 1)
+        for r in range(ROUNDS):
+            m0 = r * TILES_PER_BANK
+            distances(r, 0)
+            if r == 0:
+                query_norms(1, QUERY_TILES)
+            quantise_values(m0 - 2)
+            turn_values(m0)
+            distances(r, 1)
+            invert_total(r - 1)
+            quantise_values(m0 - 1)
+            turn_values(m0 + 1)
+            normalise(r - 1, 0)
+            normalise(r - 1, 1)
+            products(r, 0)
+            distances(r, 2)
+            distances(r, 3)
+            quantise_values(m0)
+            turn_values(m0 + 2)
+            turn_affinity(r - 1, 0)
+            maximum(r)
+            turn_affinity(r - 1, 1)
+            products(r, 1)
+            turn_values(m0 + 3)
+            exponentials(r)
+            quantise_affinity(r - 1, 0)
+            quantise_affinity(r - 1, 1)
+            quantise_values(m0 + 1)
+            products(r, 2)
+            products(r, 3)

@@ -35,7 +35,7 @@ FLOPS = 2 * VALUE_CHANNELS * MEMORY * QUERIES + 2 * 2 * KEY_CHANNELS * MEMORY * 
 
 
 def pass_order(columns):
-    return columns.rearrange("c (q t) -> c t q", t=PACK)
+    return columns.rearrange("c (q u e) -> c u q e", u=2, e=2)
 
 
 def tile_vidsam_pa_kernel(
@@ -103,8 +103,6 @@ def tile_vidsam_pa_kernel(
         nc.vector.tensor_copy(out=shrink_row[0:1, :], in_=shrink_in[:])
         ident_f32 = const.tile([P, P], F32)
         make_identity(nc, ident_f32[:])
-        ident_bf16 = const.tile([P, P], BF16)
-        make_identity(nc, ident_bf16[:])
 
         qs_m2 = const.tile([P, QUERIES], BF16)
         nc.vector.tensor_scalar(out=qs_m2[:], in0=qs[:], scalar1=-2.0, scalar2=None, op0=ALU.mult)
@@ -143,11 +141,11 @@ def tile_vidsam_pa_kernel(
 
         def spread_shrinkage(g):
             cols = slice(g * K_PASS, (g + 1) * K_PASS)
-            spread = psum_tr.tile([P, PACK, P], F32, tag="turned")
+            spread = psum_tr.tile([P, 2, P, 2], F32, tag="turned")
             nc.tensor.matmul(
                 out=spread[:], lhsT=ones_bf16[:], rhs=pass_order(shrink_row[:, cols]), start=True, stop=True
             )
-            nc.scalar.mul(out=factor[:, cols], in_=spread[:].rearrange("p t q -> p (t q)"), mul=-INV_SQRT_CK)
+            nc.scalar.mul(out=factor[:, cols], in_=spread[:].rearrange("p u q e -> p (u q e)"), mul=-INV_SQRT_CK)
 
         def distances(i, g):
             if not 0 <= i < QUERY_TILES:
@@ -155,7 +153,7 @@ def tile_vidsam_pa_kernel(
             if g == 0:
                 scaled[i] = work.tile([P, MEMORY], F32, name="scaled")
             cols = slice(g * K_PASS, (g + 1) * K_PASS)
-            dist = psum_sim.tile([P, PACK, P], F32, tag="sim")
+            dist = psum_sim.tile([P, 2, P, 2], F32, tag="sim")
             nc.tensor.matmul(
                 out=dist[:], lhsT=qe[:, i * P : (i + 1) * P], rhs=pass_order(mksq[:, cols]), start=True, stop=False
             )
@@ -164,7 +162,7 @@ def tile_vidsam_pa_kernel(
             )
             nc.vector.scalar_tensor_tensor(
                 out=scaled[i][:, cols],
-                in0=dist[:].rearrange("p t q -> p (t q)"),
+                in0=dist[:].rearrange("p u q e -> p (u q e)"),
                 scalar=b_sq[:, i : i + 1],
                 in1=factor[:, cols],
                 op0=ALU.add,
@@ -210,15 +208,16 @@ def tile_vidsam_pa_kernel(
             if not 0 <= i < QUERY_TILES:
                 return
             if half == 0:
-                aff_grouped[i] = work.tile([P, PASSES, P, PACK], BF16, name="aff_grouped", align_bytes=64)
-            turned = psum_tr.tile([P, 2, PACK, P], BF16, tag="turned")
+                aff_grouped[i] = work.tile([P, PASSES, P, 2], F32, name="aff_grouped", align_bytes=64)
+            words = aff[i][:].bitcast(F32)
+            turned = psum_tr.tile([P, 2, 2, P], F32, tag="turned")
             for gl in range(2):
-                for t in range(PACK):
-                    first = (2 * half + gl) * K_PASS + t * P
-                    nc.tensor.transpose(turned[:, gl, t, :], aff[i][:, first : first + P], ident_bf16[:])
+                for u in range(2):
+                    first = ((2 * half + gl) * 2 + u) * P
+                    nc.tensor.transpose(turned[:, gl, u, :], words[:, first : first + P], ident_f32[:])
             nc.scalar.copy(
                 out=aff_grouped[i][:, 2 * half : 2 * half + 2, :, :],
-                in_=turned[:].rearrange("q g t p -> q g p t"),
+                in_=turned[:].rearrange("q g u p -> q g p u"),
             )
 
         def quantise_affinity(i, half):
@@ -228,7 +227,7 @@ def tile_vidsam_pa_kernel(
             nc.vector.quantize_mx(
                 out=aff_codes[:, i, two, :].rearrange("q g p -> q (g p)").bitcast(FP8X4),
                 scales=aff_scales[:, i, two, :].rearrange("q g p -> q (g p)"),
-                in_=aff_grouped[i][:, two, :, :].rearrange("q g p t -> q (g p t)"),
+                in_=aff_grouped[i][:, two, :, :].rearrange("q g p u -> q (g p u)").bitcast(BF16),
             )
 
         def turn_values(m):

@@ -24,10 +24,11 @@ PASSES = MEMORY // K_PASS
 HALF = MEMORY // 2
 QUERY_TILES = QUERIES // P
 VALUE_TILES = VALUE_CHANNELS // P
+PSUM_BANKS = 8
 BANK = 512
 TILES_PER_BANK = BANK // P
 VALUE_BANKS = VALUE_TILES // TILES_PER_BANK
-ROUNDS = QUERY_TILES + 2
+VALUES_PER_ROUND = VALUE_TILES // QUERY_TILES
 
 INV_SQRT_CK = 1.0 / math.sqrt(KEY_CHANNELS)
 
@@ -56,26 +57,23 @@ def tile_vidsam_pa_kernel(
         work = stack.enter_context(tc.tile_pool(name="work", bufs=2))
         small = stack.enter_context(tc.tile_pool(name="small", bufs=4))
         stage = stack.enter_context(tc.tile_pool(name="stage", bufs=4))
-        psum_sim = stack.enter_context(tc.psum_pool(name="psum_sim", bufs=2))
-        psum_tr = stack.enter_context(tc.psum_pool(name="psum_tr", bufs=4))
-        psum_acc = stack.enter_context(tc.psum_pool(name="psum_acc", bufs=2))
+        psum = stack.enter_context(tc.psum_pool(name="psum", bufs=PSUM_BANKS))
         stack.enter_context(tc.manual_schedule())
 
         shrink_in = const.tile([1, MEMORY], BF16)
         nc.sync.dma_start(out=shrink_in[:], in_=memory_shrinkage)
         qs = const.tile([P, QUERIES], BF16)
         nc.sync.dma_start(out=qs[:], in_=query_key_sel.flatten_outer_dims())
-        qk = const.tile([P, QUERIES], BF16)
-        nc.sync.dma_start(out=qk[:], in_=query_key.flatten_outer_dims())
         qe = const.tile([P, QUERIES], BF16)
         nc.sync.dma_start(out=qe[:], in_=query_selection.flatten_outer_dims())
+        qk = const.tile([P, QUERIES], BF16)
         mksq = const.tile([P, MEMORY], BF16)
         mk = const.tile([P, MEMORY], BF16)
         values = memory_value.flatten_outer_dims()
         raw_tiles = []
 
-        def load_keys(h):
-            cols = slice(h * HALF, (h + 1) * HALF)
+        def load_keys(first, last):
+            cols = slice(first * K_PASS, last * K_PASS)
             nc.sync.dma_start(out=mksq[:, cols], in_=memory_key_sq.flatten_outer_dims()[:, cols])
             nc.sync.dma_start(out=mk[:, cols], in_=memory_key.flatten_outer_dims()[:, cols])
 
@@ -84,10 +82,11 @@ def tile_vidsam_pa_kernel(
             nc.sync.dma_start(out=raw[:], in_=values[m * P : (m + 1) * P, :])
             raw_tiles.append(raw)
 
-        load_keys(0)
-        load_values(0)
-        load_keys(1)
-        for m in range(1, VALUE_TILES):
+        load_keys(0, 1)
+        nc.sync.dma_start(out=qk[:], in_=query_key.flatten_outer_dims())
+        load_keys(1, 2)
+        load_keys(2, 4)
+        for m in range(VALUE_TILES):
             load_values(m)
 
         shrink_row = const.tile([P, MEMORY], BF16)
@@ -118,6 +117,7 @@ def tile_vidsam_pa_kernel(
         aff_scales = const.tile([P, QUERY_TILES, PASSES, P], U8, align_bytes=64)
         out_view = out.flatten_outer_dims().rearrange("(m c) p -> c m p", c=P)
 
+        dist = {}
         scaled = {}
         shift = {}
         expo = {}
@@ -128,7 +128,7 @@ def tile_vidsam_pa_kernel(
         value_grouped = {}
 
         def query_norms(first, last):
-            b_sq_bank = psum_acc.tile([P, QUERY_TILES, 2], F32, tag="acc")
+            b_sq_bank = psum.tile([P, QUERY_TILES, 2], F32, tag="bank")
             for i in range(first, last):
                 nc.tensor.matmul(
                     out=b_sq_bank[:, i, :],
@@ -141,7 +141,7 @@ def tile_vidsam_pa_kernel(
 
         def spread_shrinkage(g):
             cols = slice(g * K_PASS, (g + 1) * K_PASS)
-            spread = psum_tr.tile([P, 2, P, 2], F32, tag="turned")
+            spread = psum.tile([P, 2, P, 2], F32, tag="bank")
             nc.tensor.matmul(
                 out=spread[:], lhsT=ones_bf16[:], rhs=pass_order(shrink_row[:, cols]), start=True, stop=True
             )
@@ -150,19 +150,25 @@ def tile_vidsam_pa_kernel(
         def distances(i, g):
             if not 0 <= i < QUERY_TILES:
                 return
+            cols = slice(g * K_PASS, (g + 1) * K_PASS)
+            bank = psum.tile([P, 2, P, 2], F32, tag="bank")
+            nc.tensor.matmul(
+                out=bank[:], lhsT=qe[:, i * P : (i + 1) * P], rhs=pass_order(mksq[:, cols]), start=True, stop=False
+            )
+            nc.tensor.matmul(
+                out=bank[:], lhsT=qs_m2[:, i * P : (i + 1) * P], rhs=pass_order(mk[:, cols]), start=False, stop=True
+            )
+            dist[i, g] = bank
+
+        def similarity(i, g):
+            if not 0 <= i < QUERY_TILES:
+                return
             if g == 0:
                 scaled[i] = work.tile([P, MEMORY], F32, name="scaled")
             cols = slice(g * K_PASS, (g + 1) * K_PASS)
-            dist = psum_sim.tile([P, 2, P, 2], F32, tag="sim")
-            nc.tensor.matmul(
-                out=dist[:], lhsT=qe[:, i * P : (i + 1) * P], rhs=pass_order(mksq[:, cols]), start=True, stop=False
-            )
-            nc.tensor.matmul(
-                out=dist[:], lhsT=qs_m2[:, i * P : (i + 1) * P], rhs=pass_order(mk[:, cols]), start=False, stop=True
-            )
             nc.vector.scalar_tensor_tensor(
                 out=scaled[i][:, cols],
-                in0=dist[:].rearrange("p u q e -> p (u q e)"),
+                in0=dist[i, g][:].rearrange("p u q e -> p (u q e)"),
                 scalar=b_sq[:, i : i + 1],
                 in1=factor[:, cols],
                 op0=ALU.add,
@@ -210,7 +216,7 @@ def tile_vidsam_pa_kernel(
             if half == 0:
                 aff_grouped[i] = work.tile([P, PASSES, P, 2], F32, name="aff_grouped", align_bytes=64)
             words = aff[i][:].bitcast(F32)
-            turned = psum_tr.tile([P, 2, 2, P], F32, tag="turned")
+            turned = psum.tile([P, 2, 2, P], F32, tag="bank")
             for gl in range(2):
                 for u in range(2):
                     first = ((2 * half + gl) * 2 + u) * P
@@ -230,13 +236,14 @@ def tile_vidsam_pa_kernel(
                 in_=aff_grouped[i][:, two, :, :].rearrange("q g p u -> q (g p u)").bitcast(BF16),
             )
 
-        def turn_values(m):
+        def turn_values(m, halves=(0, 1)):
             if not 0 <= m < VALUE_TILES:
                 return
             words = raw_tiles[m][:].bitcast(F32)
-            value_grouped[m] = stage.tile([P, PASSES, P, 2], F32, name="value_grouped", align_bytes=64)
-            for half in range(2):
-                turned = psum_tr.tile([P, 2, 2, P], F32, tag="turned")
+            if 0 in halves:
+                value_grouped[m] = stage.tile([P, PASSES, P, 2], F32, name="value_grouped", align_bytes=64)
+            for half in halves:
+                turned = psum.tile([P, 2, 2, P], F32, tag="bank")
                 for gl in range(2):
                     for u in range(2):
                         first = (2 * half + gl) * 2 * P + u
@@ -258,7 +265,7 @@ def tile_vidsam_pa_kernel(
             )
 
         def product(i, b, copy_engine):
-            acc = psum_acc.tile([P, TILES_PER_BANK, P], F32, tag="acc")
+            acc = psum.tile([P, TILES_PER_BANK, P], F32, tag="bank")
             for cell in range(TILES_PER_BANK):
                 m = b * TILES_PER_BANK + cell
                 for g in range(PASSES):
@@ -281,41 +288,41 @@ def tile_vidsam_pa_kernel(
                 in_=result[:],
             )
 
-        def products(r, k):
-            due = sorted((b, i) for i in range(QUERY_TILES) for b in range(VALUE_BANKS) if max(i + 2, b + 1) == r)
-            if k < len(due):
-                b, i = due[k]
-                product(i, b, "scalar" if k == 0 else "vector")
-
         for g in range(PASSES):
             spread_shrinkage(g)
         query_norms(0, 1)
-        for r in range(ROUNDS):
-            m0 = r * TILES_PER_BANK
-            distances(r, 0)
-            if r == 0:
+        for g in range(PASSES):
+            distances(0, g)
+        for i in range(QUERY_TILES + 1):
+            m = VALUES_PER_ROUND * i
+            for g in range(PASSES):
+                similarity(i, g)
+            if i == 0:
                 query_norms(1, QUERY_TILES)
-            quantise_values(m0 - 2)
-            turn_values(m0)
-            distances(r, 1)
-            invert_total(r - 1)
-            quantise_values(m0 - 1)
-            turn_values(m0 + 1)
-            normalise(r - 1, 0)
-            normalise(r - 1, 1)
-            products(r, 0)
-            distances(r, 2)
-            distances(r, 3)
-            quantise_values(m0)
-            turn_values(m0 + 2)
-            turn_affinity(r - 1, 0)
-            maximum(r)
-            turn_affinity(r - 1, 1)
-            products(r, 1)
-            turn_values(m0 + 3)
-            exponentials(r)
-            quantise_affinity(r - 1, 0)
-            quantise_affinity(r - 1, 1)
-            quantise_values(m0 + 1)
-            products(r, 2)
-            products(r, 3)
+            turn_values(m)
+            turn_values(m + 1)
+            invert_total(i - 1)
+            quantise_values(m - 2)
+            normalise(i - 1, 0)
+            normalise(i - 1, 1)
+            for b in range(VALUE_BANKS - 1):
+                for q in range(QUERY_TILES - 1):
+                    if min(q + b + 2, QUERY_TILES) == i:
+                        product(q, b, "scalar")
+            turn_affinity(i - 1, 0)
+            turn_affinity(i - 1, 1)
+            maximum(i)
+            exponentials(i)
+            for g in range(PASSES):
+                distances(i + 1, g)
+            quantise_values(m - 1)
+            if i == QUERY_TILES:
+                for q in range(QUERY_TILES - 1):
+                    product(q, VALUE_BANKS - 1, "scalar")
+            turn_values(m + 2)
+            quantise_affinity(i - 1, 0)
+            quantise_affinity(i - 1, 1)
+            quantise_values(m)
+        product(QUERY_TILES - 1, 0, "scalar")
+        product(QUERY_TILES - 1, 1, "vector")
+        product(QUERY_TILES - 1, 2, "scalar")

@@ -24,13 +24,14 @@ PASSES = MEMORY // K_PASS
 HALF = MEMORY // 2
 QUERY_TILES = QUERIES // P
 VALUE_TILES = VALUE_CHANNELS // P
-PSUM_BANKS = 8
 BANK = 512
 TILES_PER_BANK = BANK // P
 VALUE_BANKS = VALUE_TILES // TILES_PER_BANK
 VALUES_PER_ROUND = VALUE_TILES // QUERY_TILES
 
 INV_SQRT_CK = 1.0 / math.sqrt(KEY_CHANNELS)
+
+WARM_UPS = 16
 
 FLOPS = 2 * VALUE_CHANNELS * MEMORY * QUERIES + 2 * 2 * KEY_CHANNELS * MEMORY * QUERIES
 
@@ -57,16 +58,21 @@ def tile_vidsam_pa_kernel(
         work = stack.enter_context(tc.tile_pool(name="work", bufs=2))
         small = stack.enter_context(tc.tile_pool(name="small", bufs=4))
         stage = stack.enter_context(tc.tile_pool(name="stage", bufs=4))
-        psum = stack.enter_context(tc.psum_pool(name="psum", bufs=PSUM_BANKS))
+        psum = stack.enter_context(tc.psum_pool(name="psum", bufs=8))
         stack.enter_context(tc.manual_schedule())
 
-        shrink_in = const.tile([1, MEMORY], BF16)
-        nc.sync.dma_start(out=shrink_in[:], in_=memory_shrinkage)
+        ones_bf16 = const.tile([P, P], BF16)
+        nc.vector.memset(ones_bf16[:], 1.0)
+        shrink_row = const.tile([P, MEMORY], BF16)
+        nc.vector.memset(shrink_row[:].bitcast(F32), 0.0)
+        nc.scalar.dma_start(out=shrink_row[0:1, :], in_=memory_shrinkage)
+
         qs = const.tile([P, QUERIES], BF16)
         nc.sync.dma_start(out=qs[:], in_=query_key_sel.flatten_outer_dims())
+        qk = const.tile([P, QUERIES], BF16)
+        nc.sync.dma_start(out=qk[:], in_=query_key.flatten_outer_dims())
         qe = const.tile([P, QUERIES], BF16)
         nc.sync.dma_start(out=qe[:], in_=query_selection.flatten_outer_dims())
-        qk = const.tile([P, QUERIES], BF16)
         mksq = const.tile([P, MEMORY], BF16)
         mk = const.tile([P, MEMORY], BF16)
         values = memory_value.flatten_outer_dims()
@@ -83,23 +89,17 @@ def tile_vidsam_pa_kernel(
             raw_tiles.append(raw)
 
         load_keys(0, 1)
-        nc.sync.dma_start(out=qk[:], in_=query_key.flatten_outer_dims())
         load_keys(1, 2)
         load_keys(2, 4)
         for m in range(VALUE_TILES):
             load_values(m)
 
-        shrink_row = const.tile([P, MEMORY], BF16)
-        nc.gpsimd.memset(shrink_row[:].bitcast(F32), 0.0)
-        ones_bf16 = const.tile([P, P], BF16)
-        nc.vector.memset(ones_bf16[:], 1.0)
         ones_f32 = const.tile([P, 2], F32)
         nc.vector.memset(ones_f32[:], 1.0)
         zero_col = const.tile([P, 1], F32)
         nc.vector.memset(zero_col[:], 0.0)
         one_col = const.tile([P, 1], F32)
         nc.scalar.activation(out=one_col[:], in_=zero_col[:], func=ACT.Exp)
-        nc.vector.tensor_copy(out=shrink_row[0:1, :], in_=shrink_in[:])
         ident_f32 = const.tile([P, P], F32)
         make_identity(nc, ident_f32[:])
 
@@ -113,8 +113,8 @@ def tile_vidsam_pa_kernel(
 
         value_codes = const.tile([P, VALUE_TILES, PASSES, P], U32, align_bytes=64)
         value_scales = const.tile([P, VALUE_TILES, PASSES, P], U8, align_bytes=64)
-        aff_codes = const.tile([P, QUERY_TILES, PASSES, P], U32, align_bytes=64)
-        aff_scales = const.tile([P, QUERY_TILES, PASSES, P], U8, align_bytes=64)
+        aff_codes = const.tile([P, PASSES, QUERIES], U32, align_bytes=64)
+        aff_scales = const.tile([P, PASSES, QUERIES], U8, align_bytes=64)
         out_view = out.flatten_outer_dims().rearrange("(m c) p -> c m p", c=P)
 
         dist = {}
@@ -229,12 +229,13 @@ def tile_vidsam_pa_kernel(
         def quantise_affinity(i, half):
             if not 0 <= i < QUERY_TILES:
                 return
-            two = slice(2 * half, 2 * half + 2)
-            nc.vector.quantize_mx(
-                out=aff_codes[:, i, two, :].rearrange("q g p -> q (g p)").bitcast(FP8X4),
-                scales=aff_scales[:, i, two, :].rearrange("q g p -> q (g p)"),
-                in_=aff_grouped[i][:, two, :, :].rearrange("q g p u -> q (g p u)").bitcast(BF16),
-            )
+            queries = slice(i * P, (i + 1) * P)
+            for g in (2 * half, 2 * half + 1):
+                nc.vector.quantize_mx(
+                    out=aff_codes[:, g, queries].bitcast(FP8X4),
+                    scales=aff_scales[:, g, queries],
+                    in_=aff_grouped[i][:, g, :, :].rearrange("q p u -> q (p u)").bitcast(BF16),
+                )
 
         def turn_values(m, halves=(0, 1)):
             if not 0 <= m < VALUE_TILES:
@@ -264,34 +265,38 @@ def tile_vidsam_pa_kernel(
                 in_=value_grouped[m][:].rearrange("q g c u -> q (g c u)").bitcast(BF16),
             )
 
-        def product(i, b, copy_engine):
-            acc = psum.tile([P, TILES_PER_BANK, P], F32, tag="bank")
-            for cell in range(TILES_PER_BANK):
-                m = b * TILES_PER_BANK + cell
+        def product(query_tile, query_tiles, value_tile, value_tiles, copy_engine):
+            queries = query_tiles * P
+            first_query = query_tile * P
+            columns = slice(first_query, first_query + queries)
+            acc = psum.tile([P, value_tiles, queries], F32, tag="bank")
+            for cell in range(value_tiles):
+                m = value_tile + cell
                 for g in range(PASSES):
                     nc.tensor.matmul_mx(
                         out=acc[:, cell, :],
                         lhsT=value_codes[:, m, g, :].bitcast(FP8X4),
                         lhsT_scale=value_scales[:, m, g, :],
-                        rhs=aff_codes[:, i, g, :].bitcast(FP8X4),
-                        rhs_scale=aff_scales[:, i, g, :],
+                        rhs=aff_codes[:, g, columns].bitcast(FP8X4),
+                        rhs_scale=aff_scales[:, g, columns],
                         start=(g == 0),
                         stop=(g == PASSES - 1),
                     )
-            result = stage.tile([P, TILES_PER_BANK, P], F32, name="result")
+            result = stage.tile([P, value_tiles, queries], F32, name="result")
             if copy_engine == "vector":
                 nc.vector.tensor_copy(out=result[:], in_=acc[:])
             else:
                 nc.scalar.copy(out=result[:], in_=acc[:])
-            nc.sync.dma_start(
-                out=out_view[:, b * TILES_PER_BANK : (b + 1) * TILES_PER_BANK, i * P : (i + 1) * P],
-                in_=result[:],
-            )
+            nc.sync.dma_start(out=out_view[:, value_tile : value_tile + value_tiles, columns], in_=result[:])
 
+        warm_up = psum.tile([P, P], F32, tag="bank")
+        for n in range(WARM_UPS):
+            nc.tensor.matmul(out=warm_up[:], lhsT=ones_bf16[:], rhs=ones_bf16[:], start=True, stop=True)
         for g in range(PASSES):
             spread_shrinkage(g)
+        distances(0, 0)
         query_norms(0, 1)
-        for g in range(PASSES):
+        for g in range(1, PASSES):
             distances(0, g)
         for i in range(QUERY_TILES + 1):
             m = VALUES_PER_ROUND * i
@@ -305,24 +310,35 @@ def tile_vidsam_pa_kernel(
             quantise_values(m - 2)
             normalise(i - 1, 0)
             normalise(i - 1, 1)
-            for b in range(VALUE_BANKS - 1):
-                for q in range(QUERY_TILES - 1):
-                    if min(q + b + 2, QUERY_TILES) == i:
-                        product(q, b, "scalar")
+            if i == 2:
+                product(0, 1, 0, 4, "scalar")
+            elif i == 3:
+                product(1, 1, 0, 4, "scalar")
+            elif i == 4:
+                product(2, 1, 0, 4, "scalar")
+                product(2, 1, 4, 4, "scalar")
             turn_affinity(i - 1, 0)
             turn_affinity(i - 1, 1)
             maximum(i)
             exponentials(i)
             for g in range(PASSES):
                 distances(i + 1, g)
-            quantise_values(m - 1)
-            if i == QUERY_TILES:
-                for q in range(QUERY_TILES - 1):
-                    product(q, VALUE_BANKS - 1, "scalar")
+            if i != 3:
+                quantise_values(m - 1)
             turn_values(m + 2)
+            if i == 3:
+                product(0, 2, 4, 2, "scalar")
+                product(0, 2, 6, 2, "scalar")
+            elif i == 4:
+                product(0, 2, 8, 2, "scalar")
+                product(0, 2, 10, 2, "scalar")
             quantise_affinity(i - 1, 0)
             quantise_affinity(i - 1, 1)
+            if i == 3:
+                quantise_values(m - 1)
             quantise_values(m)
-        product(QUERY_TILES - 1, 0, "scalar")
-        product(QUERY_TILES - 1, 1, "vector")
-        product(QUERY_TILES - 1, 2, "scalar")
+        product(3, 1, 0, 4, "scalar")
+        product(3, 1, 4, 4, "vector")
+        product(2, 2, 8, 2, "scalar")
+        product(2, 2, 10, 1, "vector")
+        product(2, 2, 11, 1, "scalar")

@@ -61,12 +61,8 @@ def tile_vidsam_pa_kernel(
         psum = stack.enter_context(tc.psum_pool(name="psum", bufs=8))
         stack.enter_context(tc.manual_schedule())
 
-        ones_bf16 = const.tile([P, P], BF16)
-        nc.vector.memset(ones_bf16[:], 1.0)
-        shrink_row = const.tile([P, MEMORY], BF16)
-        nc.vector.memset(shrink_row[:].bitcast(F32), 0.0)
-        nc.scalar.dma_start(out=shrink_row[0:1, :], in_=memory_shrinkage)
-
+        shrink_in = const.tile([1, MEMORY], BF16)
+        nc.sync.dma_start(out=shrink_in[:], in_=memory_shrinkage)
         qs = const.tile([P, QUERIES], BF16)
         nc.sync.dma_start(out=qs[:], in_=query_key_sel.flatten_outer_dims())
         qk = const.tile([P, QUERIES], BF16)
@@ -94,12 +90,17 @@ def tile_vidsam_pa_kernel(
         for m in range(VALUE_TILES):
             load_values(m)
 
+        shrink_row = const.tile([P, MEMORY], BF16)
+        nc.gpsimd.memset(shrink_row[:].bitcast(F32), 0.0)
+        ones_bf16 = const.tile([P, P], BF16)
+        nc.vector.memset(ones_bf16[:], 1.0)
         ones_f32 = const.tile([P, 2], F32)
         nc.vector.memset(ones_f32[:], 1.0)
         zero_col = const.tile([P, 1], F32)
         nc.vector.memset(zero_col[:], 0.0)
         one_col = const.tile([P, 1], F32)
         nc.scalar.activation(out=one_col[:], in_=zero_col[:], func=ACT.Exp)
+        nc.vector.tensor_copy(out=shrink_row[0:1, :], in_=shrink_in[:])
         ident_f32 = const.tile([P, P], F32)
         make_identity(nc, ident_f32[:])
 
@@ -305,11 +306,10 @@ def tile_vidsam_pa_kernel(
             if i == 0:
                 query_norms(1, QUERY_TILES)
             turn_values(m)
+            distances(i + 1, 0)
+            if i == 3:
+                product(0, 2, 4, 2, "scalar")
             turn_values(m + 1)
-            invert_total(i - 1)
-            quantise_values(m - 2)
-            normalise(i - 1, 0)
-            normalise(i - 1, 1)
             if i == 2:
                 product(0, 1, 0, 4, "scalar")
             elif i == 3:
@@ -317,25 +317,26 @@ def tile_vidsam_pa_kernel(
             elif i == 4:
                 product(2, 1, 0, 4, "scalar")
                 product(2, 1, 4, 4, "scalar")
+            invert_total(i - 1)
+            quantise_values(m - 2)
+            normalise(i - 1, 0)
+            normalise(i - 1, 1)
             turn_affinity(i - 1, 0)
             turn_affinity(i - 1, 1)
             maximum(i)
             exponentials(i)
-            for g in range(PASSES):
-                distances(i + 1, g)
-            if i != 3:
-                quantise_values(m - 1)
+            distances(i + 1, 1)
             turn_values(m + 2)
+            distances(i + 1, 2)
+            distances(i + 1, 3)
+            quantise_values(m - 1)
             if i == 3:
-                product(0, 2, 4, 2, "scalar")
                 product(0, 2, 6, 2, "scalar")
             elif i == 4:
                 product(0, 2, 8, 2, "scalar")
                 product(0, 2, 10, 2, "scalar")
             quantise_affinity(i - 1, 0)
             quantise_affinity(i - 1, 1)
-            if i == 3:
-                quantise_values(m - 1)
             quantise_values(m)
         product(3, 1, 0, 4, "scalar")
         product(3, 1, 4, 4, "vector")

@@ -58,6 +58,7 @@ def tile_vidsam_pa_kernel(
         work = stack.enter_context(tc.tile_pool(name="work", bufs=2))
         small = stack.enter_context(tc.tile_pool(name="small", bufs=4))
         stage = stack.enter_context(tc.tile_pool(name="stage", bufs=4))
+        results = stack.enter_context(tc.tile_pool(name="results", bufs=8))
         psum = stack.enter_context(tc.psum_pool(name="psum", bufs=8))
         stack.enter_context(tc.manual_schedule())
 
@@ -65,8 +66,6 @@ def tile_vidsam_pa_kernel(
         nc.sync.dma_start(out=shrink_in[:], in_=memory_shrinkage)
         qs = const.tile([P, QUERIES], BF16)
         nc.sync.dma_start(out=qs[:], in_=query_key_sel.flatten_outer_dims())
-        qk = const.tile([P, QUERIES], BF16)
-        nc.sync.dma_start(out=qk[:], in_=query_key.flatten_outer_dims())
         qe = const.tile([P, QUERIES], BF16)
         nc.sync.dma_start(out=qe[:], in_=query_selection.flatten_outer_dims())
         mksq = const.tile([P, MEMORY], BF16)
@@ -85,6 +84,8 @@ def tile_vidsam_pa_kernel(
             raw_tiles.append(raw)
 
         load_keys(0, 1)
+        qk = const.tile([P, QUERIES], BF16)
+        nc.sync.dma_start(out=qk[:], in_=query_key.flatten_outer_dims())
         load_keys(1, 2)
         load_keys(2, 4)
         for m in range(VALUE_TILES):
@@ -100,7 +101,9 @@ def tile_vidsam_pa_kernel(
         nc.vector.memset(zero_col[:], 0.0)
         one_col = const.tile([P, 1], F32)
         nc.scalar.activation(out=one_col[:], in_=zero_col[:], func=ACT.Exp)
-        nc.vector.tensor_copy(out=shrink_row[0:1, :], in_=shrink_in[:])
+        for g in range(PASSES):
+            cols = slice(g * K_PASS, (g + 1) * K_PASS)
+            nc.vector.tensor_copy(out=shrink_row[0:1, cols], in_=shrink_in[:, cols])
         ident_f32 = const.tile([P, P], F32)
         make_identity(nc, ident_f32[:])
 
@@ -127,6 +130,7 @@ def tile_vidsam_pa_kernel(
         aff = {}
         aff_grouped = {}
         value_grouped = {}
+        sums = {}
 
         def query_norms(first, last):
             b_sq_bank = psum.tile([P, QUERY_TILES, 2], F32, tag="bank")
@@ -266,7 +270,7 @@ def tile_vidsam_pa_kernel(
                 in_=value_grouped[m][:].rearrange("q g c u -> q (g c u)").bitcast(BF16),
             )
 
-        def product(query_tile, query_tiles, value_tile, value_tiles, copy_engine):
+        def product(query_tile, query_tiles, value_tile, value_tiles):
             queries = query_tiles * P
             first_query = query_tile * P
             columns = slice(first_query, first_query + queries)
@@ -283,7 +287,11 @@ def tile_vidsam_pa_kernel(
                         start=(g == 0),
                         stop=(g == PASSES - 1),
                     )
-            result = stage.tile([P, value_tiles, queries], F32, name="result")
+            sums[query_tile, value_tile] = (acc, columns, value_tiles, queries)
+
+        def store(query_tile, value_tile, copy_engine):
+            acc, columns, value_tiles, queries = sums[query_tile, value_tile]
+            result = results.tile([P, value_tiles, queries], F32, name="result")
             if copy_engine == "vector":
                 nc.vector.tensor_copy(out=result[:], in_=acc[:])
             else:
@@ -295,9 +303,8 @@ def tile_vidsam_pa_kernel(
             nc.tensor.matmul(out=warm_up[:], lhsT=ones_bf16[:], rhs=ones_bf16[:], start=True, stop=True)
         for g in range(PASSES):
             spread_shrinkage(g)
-        distances(0, 0)
         query_norms(0, 1)
-        for g in range(1, PASSES):
+        for g in range(PASSES):
             distances(0, g)
         for i in range(QUERY_TILES + 1):
             m = VALUES_PER_ROUND * i
@@ -308,38 +315,60 @@ def tile_vidsam_pa_kernel(
             turn_values(m)
             distances(i + 1, 0)
             if i == 3:
-                product(0, 2, 4, 2, "scalar")
+                product(0, 2, 4, 2)
+                store(0, 4, "scalar")
             turn_values(m + 1)
             if i == 2:
-                product(0, 1, 0, 4, "scalar")
+                product(0, 1, 0, 4)
+                store(0, 0, "scalar")
             elif i == 3:
-                product(1, 1, 0, 4, "scalar")
+                product(1, 1, 0, 4)
+                store(1, 0, "scalar")
             elif i == 4:
-                product(2, 1, 0, 4, "scalar")
-                product(2, 1, 4, 4, "scalar")
+                product(2, 1, 0, 4)
+                store(2, 0, "scalar")
+                product(2, 1, 4, 4)
+                store(2, 4, "scalar")
+                product(0, 2, 8, 2)
             invert_total(i - 1)
-            quantise_values(m - 2)
+            if i < QUERY_TILES:
+                quantise_values(m - 2)
             normalise(i - 1, 0)
             normalise(i - 1, 1)
             turn_affinity(i - 1, 0)
             turn_affinity(i - 1, 1)
+            if i == QUERY_TILES:
+                store(0, 8, "scalar")
+                quantise_values(m - 2)
             maximum(i)
             exponentials(i)
             distances(i + 1, 1)
             turn_values(m + 2)
             distances(i + 1, 2)
             distances(i + 1, 3)
-            quantise_values(m - 1)
+            if i != 3:
+                quantise_values(m - 1)
             if i == 3:
-                product(0, 2, 6, 2, "scalar")
+                product(0, 2, 6, 2)
             elif i == 4:
-                product(0, 2, 8, 2, "scalar")
-                product(0, 2, 10, 2, "scalar")
+                product(0, 2, 10, 2)
+                store(0, 10, "scalar")
+                product(2, 1, 8, 2)
+                store(2, 8, "scalar")
             quantise_affinity(i - 1, 0)
             quantise_affinity(i - 1, 1)
+            if i == 3:
+                quantise_values(m - 1)
             quantise_values(m)
-        product(3, 1, 0, 4, "scalar")
-        product(3, 1, 4, 4, "vector")
-        product(2, 2, 8, 2, "scalar")
-        product(2, 2, 10, 1, "vector")
-        product(2, 2, 11, 1, "scalar")
+            if i == 3:
+                store(0, 6, "vector")
+        product(3, 1, 0, 4)
+        store(3, 0, "scalar")
+        product(3, 1, 4, 4)
+        store(3, 4, "vector")
+        product(3, 1, 8, 2)
+        store(3, 8, "scalar")
+        product(2, 2, 10, 1)
+        store(2, 10, "vector")
+        product(2, 2, 11, 1)
+        store(2, 11, "scalar")

@@ -29,6 +29,9 @@ TILES_PER_BANK = BANK // P
 VALUE_BANKS = VALUE_TILES // TILES_PER_BANK
 VALUES_PER_ROUND = VALUE_TILES // QUERY_TILES
 
+FIRST = slice(0, P)
+REST = slice(P, QUERIES)
+
 INV_SQRT_CK = 1.0 / math.sqrt(KEY_CHANNELS)
 
 WARM_UPS = 16
@@ -65,31 +68,41 @@ def tile_vidsam_pa_kernel(
         shrink_in = const.tile([1, MEMORY], BF16)
         nc.sync.dma_start(out=shrink_in[:], in_=memory_shrinkage)
         qs = const.tile([P, QUERIES], BF16)
-        nc.sync.dma_start(out=qs[:], in_=query_key_sel.flatten_outer_dims())
         qe = const.tile([P, QUERIES], BF16)
-        nc.sync.dma_start(out=qe[:], in_=query_selection.flatten_outer_dims())
+        qk = const.tile([P, QUERIES], BF16)
         mksq = const.tile([P, MEMORY], BF16)
         mk = const.tile([P, MEMORY], BF16)
         values = memory_value.flatten_outer_dims()
         raw_tiles = []
+
+        def load_queries(tile, source, cols):
+            nc.sync.dma_start(out=tile[:, cols], in_=source.flatten_outer_dims()[:, cols])
 
         def load_keys(first, last):
             cols = slice(first * K_PASS, last * K_PASS)
             nc.sync.dma_start(out=mksq[:, cols], in_=memory_key_sq.flatten_outer_dims()[:, cols])
             nc.sync.dma_start(out=mk[:, cols], in_=memory_key.flatten_outer_dims()[:, cols])
 
-        def load_values(m):
+        def load_values(m, parts):
             raw = raw_pool.tile([P, MEMORY], BF16, name="raw")
-            nc.sync.dma_start(out=raw[:], in_=values[m * P : (m + 1) * P, :])
+            width = MEMORY // parts
+            for first in range(0, MEMORY, width):
+                cols = slice(first, first + width)
+                nc.sync.dma_start(out=raw[:, cols], in_=values[m * P : (m + 1) * P, cols])
             raw_tiles.append(raw)
 
+        load_queries(qs, query_key_sel, FIRST)
+        load_queries(qe, query_selection, FIRST)
         load_keys(0, 1)
-        qk = const.tile([P, QUERIES], BF16)
-        nc.sync.dma_start(out=qk[:], in_=query_key.flatten_outer_dims())
+        load_queries(qk, query_key, FIRST)
         load_keys(1, 2)
         load_keys(2, 4)
-        for m in range(VALUE_TILES):
-            load_values(m)
+        load_values(0, 2)
+        load_queries(qs, query_key_sel, REST)
+        load_queries(qe, query_selection, REST)
+        load_queries(qk, query_key, REST)
+        for m in range(1, VALUE_TILES):
+            load_values(m, 1)
 
         shrink_row = const.tile([P, MEMORY], BF16)
         nc.gpsimd.memset(shrink_row[:].bitcast(F32), 0.0)
@@ -108,10 +121,7 @@ def tile_vidsam_pa_kernel(
         make_identity(nc, ident_f32[:])
 
         qs_m2 = const.tile([P, QUERIES], BF16)
-        nc.vector.tensor_scalar(out=qs_m2[:], in0=qs[:], scalar1=-2.0, scalar2=None, op0=ALU.mult)
         qs_qk = const.tile([P, QUERIES], F32)
-        nc.vector.tensor_tensor(out=qs_qk[:, 0:P], in0=qs[:, 0:P], in1=qk[:, 0:P], op=ALU.mult)
-        nc.vector.tensor_tensor(out=qs_qk[:, P:], in0=qs[:, P:], in1=qk[:, P:], op=ALU.mult)
         b_sq = const.tile([P, QUERY_TILES], F32)
         factor = const.tile([P, MEMORY], F32)
 
@@ -131,6 +141,12 @@ def tile_vidsam_pa_kernel(
         aff_grouped = {}
         value_grouped = {}
         sums = {}
+
+        def prepare_queries(engine, cols):
+            engine.tensor_scalar(
+                out=qs_m2[:, cols], in0=qs[:, cols], scalar1=-2.0, scalar2=1.0, op0=ALU.mult, op1=ALU.mult
+            )
+            engine.tensor_tensor(out=qs_qk[:, cols], in0=qs[:, cols], in1=qk[:, cols], op=ALU.mult)
 
         def query_norms(first, last):
             b_sq_bank = psum.tile([P, QUERY_TILES, 2], F32, tag="bank")
@@ -303,6 +319,8 @@ def tile_vidsam_pa_kernel(
             nc.tensor.matmul(out=warm_up[:], lhsT=ones_bf16[:], rhs=ones_bf16[:], start=True, stop=True)
         for g in range(PASSES):
             spread_shrinkage(g)
+        prepare_queries(nc.vector, FIRST)
+        prepare_queries(nc.gpsimd, REST)
         query_norms(0, 1)
         for g in range(PASSES):
             distances(0, g)
@@ -310,8 +328,6 @@ def tile_vidsam_pa_kernel(
             m = VALUES_PER_ROUND * i
             for g in range(PASSES):
                 similarity(i, g)
-            if i == 0:
-                query_norms(1, QUERY_TILES)
             turn_values(m)
             distances(i + 1, 0)
             if i == 3:
@@ -342,15 +358,17 @@ def tile_vidsam_pa_kernel(
                 quantise_values(m - 2)
             maximum(i)
             exponentials(i)
+            if i == 0:
+                query_norms(1, QUERY_TILES)
             distances(i + 1, 1)
+            if i == 3:
+                product(0, 2, 6, 2)
             turn_values(m + 2)
             distances(i + 1, 2)
             distances(i + 1, 3)
             if i != 3:
                 quantise_values(m - 1)
-            if i == 3:
-                product(0, 2, 6, 2)
-            elif i == 4:
+            if i == 4:
                 product(0, 2, 10, 2)
                 store(0, 10, "scalar")
                 product(2, 1, 8, 2)

@@ -337,6 +337,7 @@ def tile_vidsam_pa_kernel(
             if i == 2:
                 product(0, 1, 0, 4)
                 store(0, 0, "scalar")
+                distances(3, 1)
             elif i == 3:
                 product(1, 1, 0, 4)
                 store(1, 0, "scalar")
@@ -360,7 +361,8 @@ def tile_vidsam_pa_kernel(
             exponentials(i)
             if i == 0:
                 query_norms(1, QUERY_TILES)
-            distances(i + 1, 1)
+            if i != 2:
+                distances(i + 1, 1)
             if i == 3:
                 product(0, 2, 6, 2)
             turn_values(m + 2)
@@ -388,5 +390,7 @@ def tile_vidsam_pa_kernel(
         store(3, 8, "scalar")
         product(2, 2, 10, 1)
         store(2, 10, "vector")
-        product(2, 2, 11, 1)
+        product(2, 1, 11, 1)
         store(2, 11, "scalar")
+        product(3, 1, 11, 1)
+        store(3, 11, "vector")

@@ -93,9 +93,8 @@ def tile_vidsam_pa_kernel(
 
         load_queries(qs, query_key_sel, FIRST)
         load_queries(qe, query_selection, FIRST)
-        load_keys(0, 1)
         load_queries(qk, query_key, FIRST)
-        load_keys(1, 2)
+        load_keys(0, 2)
         load_keys(2, 4)
         load_values(0, 2)
         load_queries(qs, query_key_sel, REST)

import math
from contextlib import ExitStack

import concourse.mybir as mybir
from concourse.masks import make_identity

F32 = mybir.dt.float32
BF16 = mybir.dt.bfloat16
U32 = mybir.dt.uint32
U8 = mybir.dt.uint8
FP8X4 = mybir.dt.float8_e4m3fn_x4
ALU = mybir.AluOpType
ACT = mybir.ActivationFunctionType
AXIS = mybir.AxisListType

P = 128
KEY_CHANNELS = 128
MEMORY = 2048
QUERIES = 512
VALUE_CHANNELS = 1536
PACK = 4
K_PASS = P * PACK
PASSES = MEMORY // K_PASS
HALF = MEMORY // 2
QUERY_TILES = QUERIES // P
VALUE_TILES = VALUE_CHANNELS // P
BANK = 512
TILES_PER_BANK = BANK // P
VALUE_BANKS = VALUE_TILES // TILES_PER_BANK
VALUES_PER_ROUND = VALUE_TILES // QUERY_TILES

FIRST = slice(0, P)
REST = slice(P, QUERIES)

INV_SQRT_CK = 1.0 / math.sqrt(KEY_CHANNELS)

WARM_UPS = 16

FLOPS = 2 * VALUE_CHANNELS * MEMORY * QUERIES + 2 * 2 * KEY_CHANNELS * MEMORY * QUERIES


def pass_order(columns):
    return columns.rearrange("c (q u e) -> c u q e", u=2, e=2)


def tile_vidsam_pa_kernel(
    tc,
    memory_key,
    memory_key_sq,
    query_key,
    query_selection,
    query_key_sel,
    memory_shrinkage,
    memory_value,
    out,
):
    nc = tc.nc
    with ExitStack() as stack:
        const = stack.enter_context(tc.tile_pool(name="const", bufs=1))
        raw_pool = stack.enter_context(tc.tile_pool(name="raw", bufs=VALUE_TILES))
        work = stack.enter_context(tc.tile_pool(name="work", bufs=2))
        small = stack.enter_context(tc.tile_pool(name="small", bufs=4))
        stage = stack.enter_context(tc.tile_pool(name="stage", bufs=4))
        results = stack.enter_context(tc.tile_pool(name="results", bufs=8))
        psum = stack.enter_context(tc.psum_pool(name="psum", bufs=8))
        stack.enter_context(tc.manual_schedule())

        shrink_in = const.tile([1, MEMORY], BF16)
        nc.sync.dma_start(out=shrink_in[:], in_=memory_shrinkage)
        qs = const.tile([P, QUERIES], BF16)
        qe = const.tile([P, QUERIES], BF16)
        qk = const.tile([P, QUERIES], BF16)
        mksq = const.tile([P, MEMORY], BF16)
        mk = const.tile([P, MEMORY], BF16)
        values = memory_value.flatten_outer_dims()
        raw_tiles = []

        def load_queries(tile, source, cols):
            nc.sync.dma_start(out=tile[:, cols], in_=source.flatten_outer_dims()[:, cols])

        def load_keys(first, last):
            cols = slice(first * K_PASS, last * K_PASS)
            nc.sync.dma_start(out=mksq[:, cols], in_=memory_key_sq.flatten_outer_dims()[:, cols])
            nc.sync.dma_start(out=mk[:, cols], in_=memory_key.flatten_outer_dims()[:, cols])

        def load_values(m, parts):
            raw = raw_pool.tile([P, MEMORY], BF16, name="raw")
            width = MEMORY // parts
            for first in range(0, MEMORY, width):
                cols = slice(first, first + width)
                nc.sync.dma_start(out=raw[:, cols], in_=values[m * P : (m + 1) * P, cols])
            raw_tiles.append(raw)

        load_queries(qs, query_key_sel, FIRST)
        load_queries(qe, query_selection, FIRST)
        load_queries(qk, query_key, FIRST)
        load_keys(0, 2)
        load_keys(2, 4)
        load_values(0, 2)
        load_queries(qs, query_key_sel, REST)
        load_queries(qe, query_selection, REST)
        load_queries(qk, query_key, REST)
        for m in range(1, VALUE_TILES):
            load_values(m, 1)

        shrink_row = const.tile([P, MEMORY], BF16)
        nc.gpsimd.memset(shrink_row[:].bitcast(F32), 0.0)
        ones_bf16 = const.tile([P, P], BF16)
        nc.vector.memset(ones_bf16[:], 1.0)
        ones_f32 = const.tile([P, 2], F32)
        nc.vector.memset(ones_f32[:], 1.0)
        zero_col = const.tile([P, 1], F32)
        nc.vector.memset(zero_col[:], 0.0)
        one_col = const.tile([P, 1], F32)
        nc.scalar.activation(out=one_col[:], in_=zero_col[:], func=ACT.Exp)
        for g in range(PASSES):
            cols = slice(g * K_PASS, (g + 1) * K_PASS)
            nc.vector.tensor_copy(out=shrink_row[0:1, cols], in_=shrink_in[:, cols])
        ident_f32 = const.tile([P, P], F32)
        make_identity(nc, ident_f32[:])

        qs_m2 = const.tile([P, QUERIES], BF16)
        qs_qk = const.tile([P, QUERIES], F32)
        b_sq = const.tile([P, QUERY_TILES], F32)
        factor = const.tile([P, MEMORY], F32)

        value_codes = const.tile([P, VALUE_TILES, PASSES, P], U32, align_bytes=64)
        value_scales = const.tile([P, VALUE_TILES, PASSES, P], U8, align_bytes=64)
        aff_codes = const.tile([P, PASSES, QUERIES], U32, align_bytes=64)
        aff_scales = const.tile([P, PASSES, QUERIES], U8, align_bytes=64)
        out_view = out.flatten_outer_dims().rearrange("(m c) p -> c m p", c=P)

        dist = {}
        scaled = {}
        shift = {}
        expo = {}
        total = {}
        inverse = {}
        aff = {}
        aff_grouped = {}
        value_grouped = {}
        sums = {}

        def prepare_queries(engine, cols):
            engine.tensor_scalar(
                out=qs_m2[:, cols], in0=qs[:, cols], scalar1=-2.0, scalar2=1.0, op0=ALU.mult, op1=ALU.mult
            )
            engine.tensor_tensor(out=qs_qk[:, cols], in0=qs[:, cols], in1=qk[:, cols], op=ALU.mult)

        def query_norms(first, last):
            b_sq_bank = psum.tile([P, QUERY_TILES, 2], F32, tag="bank")
            for i in range(first, last):
                nc.tensor.matmul(
                    out=b_sq_bank[:, i, :],
                    lhsT=qs_qk[:, i * P : (i + 1) * P],
                    rhs=ones_f32[:],
                    start=True,
                    stop=True,
                )
            nc.vector.tensor_copy(out=b_sq[:, first:last], in_=b_sq_bank[:, first:last, 0])

        def spread_shrinkage(g):
            cols = slice(g * K_PASS, (g + 1) * K_PASS)
            spread = psum.tile([P, 2, P, 2], F32, tag="bank")
            nc.tensor.matmul(
                out=spread[:], lhsT=ones_bf16[:], rhs=pass_order(shrink_row[:, cols]), start=True, stop=True
            )
            nc.scalar.mul(out=factor[:, cols], in_=spread[:].rearrange("p u q e -> p (u q e)"), mul=-INV_SQRT_CK)

        def distances(i, g):
            if not 0 <= i < QUERY_TILES:
                return
            cols = slice(g * K_PASS, (g + 1) * K_PASS)
            bank = psum.tile([P, 2, P, 2], F32, tag="bank")
            nc.tensor.matmul(
                out=bank[:], lhsT=qe[:, i * P : (i + 1) * P], rhs=pass_order(mksq[:, cols]), start=True, stop=False
            )
            nc.tensor.matmul(
                out=bank[:], lhsT=qs_m2[:, i * P : (i + 1) * P], rhs=pass_order(mk[:, cols]), start=False, stop=True
            )
            dist[i, g] = bank

        def similarity(i, g):
            if not 0 <= i < QUERY_TILES:
                return
            if g == 0:
                scaled[i] = work.tile([P, MEMORY], F32, name="scaled")
            cols = slice(g * K_PASS, (g + 1) * K_PASS)
            nc.vector.scalar_tensor_tensor(
                out=scaled[i][:, cols],
                in0=dist[i, g][:].rearrange("p u q e -> p (u q e)"),
                scalar=b_sq[:, i : i + 1],
                in1=factor[:, cols],
                op0=ALU.add,
                op1=ALU.mult,
            )

        def maximum(i):
            if not 0 <= i < QUERY_TILES:
                return
            shift[i] = small.tile([P, 1], F32, name="shift")
            nc.vector.tensor_reduce(out=shift[i][:], in_=scaled[i][:], axis=AXIS.X, op=ALU.max, negate=True)

        def exponentials(i):
            if not 0 <= i < QUERY_TILES:
                return
            expo[i] = work.tile([P, MEMORY], F32, name="expo")
            total[i] = small.tile([P, 1], F32, name="total")
            nc.scalar.activation(
                out=expo[i][:],
                in_=scaled[i][:],
                func=ACT.Exp,
                bias=shift[i][:],
                accum_out=total[i][:],
            )

        def invert_total(i):
            if not 0 <= i < QUERY_TILES:
                return
            inverse[i] = small.tile([P, 1], F32, name="inverse")
            nc.vector.reciprocal(out=inverse[i][:], in_=total[i][:])

        def normalise(i, half):
            if not 0 <= i < QUERY_TILES:
                return
            if half == 0:
                aff[i] = work.tile([P, MEMORY], BF16, name="aff")
            cols = slice(half * HALF, (half + 1) * HALF)
            nc.vector.tensor_scalar(
                out=aff[i][:, cols], in0=expo[i][:, cols], scalar1=inverse[i][:], scalar2=None, op0=ALU.mult
            )

        def turn_affinity(i, half):
            if not 0 <= i < QUERY_TILES:
                return
            if half == 0:
                aff_grouped[i] = work.tile([P, PASSES, P, 2], F32, name="aff_grouped", align_bytes=64)
            words = aff[i][:].bitcast(F32)
            turned = psum.tile([P, 2, 2, P], F32, tag="bank")
            for gl in range(2):
                for u in range(2):
                    first = ((2 * half + gl) * 2 + u) * P
                    nc.tensor.transpose(turned[:, gl, u, :], words[:, first : first + P], ident_f32[:])
            nc.scalar.copy(
                out=aff_grouped[i][:, 2 * half : 2 * half + 2, :, :],
                in_=turned[:].rearrange("q g u p -> q g p u"),
            )

        def quantise_affinity(i, half):
            if not 0 <= i < QUERY_TILES:
                return
            queries = slice(i * P, (i + 1) * P)
            for g in (2 * half, 2 * half + 1):
                nc.vector.quantize_mx(
                    out=aff_codes[:, g, queries].bitcast(FP8X4),
                    scales=aff_scales[:, g, queries],
                    in_=aff_grouped[i][:, g, :, :].rearrange("q p u -> q (p u)").bitcast(BF16),
                )

        def turn_values(m, halves=(0, 1)):
            if not 0 <= m < VALUE_TILES:
                return
            words = raw_tiles[m][:].bitcast(F32)
            if 0 in halves:
                value_grouped[m] = stage.tile([P, PASSES, P, 2], F32, name="value_grouped", align_bytes=64)
            for half in halves:
                turned = psum.tile([P, 2, 2, P], F32, tag="bank")
                for gl in range(2):
                    for u in range(2):
                        first = (2 * half + gl) * 2 * P + u
                        nc.tensor.transpose(
                            turned[:, gl, u, :], words[:, first : first + 2 * P - 1 : 2], ident_f32[:]
                        )
                nc.scalar.copy(
                    out=value_grouped[m][:, 2 * half : 2 * half + 2, :, :],
                    in_=turned[:].rearrange("q g u c -> q g c u"),
                )

        def quantise_values(m):
            if not 0 <= m < VALUE_TILES:
                return
            nc.vector.quantize_mx(
                out=value_codes[:, m, :, :].rearrange("q g c -> q (g c)").bitcast(FP8X4),
                scales=value_scales[:, m, :, :].rearrange("q g c -> q (g c)"),
                in_=value_grouped[m][:].rearrange("q g c u -> q (g c u)").bitcast(BF16),
            )

        def product(query_tile, query_tiles, value_tile, value_tiles):
            queries = query_tiles * P
            first_query = query_tile * P
            columns = slice(first_query, first_query + queries)
            acc = psum.tile([P, value_tiles, queries], F32, tag="bank")
            for cell in range(value_tiles):
                m = value_tile + cell
                for g in range(PASSES):
                    nc.tensor.matmul_mx(
                        out=acc[:, cell, :],
                        lhsT=value_codes[:, m, g, :].bitcast(FP8X4),
                        lhsT_scale=value_scales[:, m, g, :],
                        rhs=aff_codes[:, g, columns].bitcast(FP8X4),
                        rhs_scale=aff_scales[:, g, columns],
                        start=(g == 0),
                        stop=(g == PASSES - 1),
                    )
            sums[query_tile, value_tile] = (acc, columns, value_tiles, queries)

        def store(query_tile, value_tile, copy_engine):
            acc, columns, value_tiles, queries = sums[query_tile, value_tile]
            result = results.tile([P, value_tiles, queries], F32, name="result")
            if copy_engine == "vector":
                nc.vector.tensor_copy(out=result[:], in_=acc[:])
            else:
                nc.scalar.copy(out=result[:], in_=acc[:])
            nc.sync.dma_start(out=out_view[:, value_tile : value_tile + value_tiles, columns], in_=result[:])

        warm_up = psum.tile([P, P], F32, tag="bank")
        for n in range(WARM_UPS):
            nc.tensor.matmul(out=warm_up[:], lhsT=ones_bf16[:], rhs=ones_bf16[:], start=True, stop=True)
        for g in range(PASSES):
            spread_shrinkage(g)
        prepare_queries(nc.vector, FIRST)
        prepare_queries(nc.gpsimd, REST)
        query_norms(0, 1)
        for g in range(PASSES):
            distances(0, g)
        for i in range(QUERY_TILES + 1):
            m = VALUES_PER_ROUND * i
            for g in range(PASSES):
                similarity(i, g)
            turn_values(m)
            distances(i + 1, 0)
            if i == 3:
                product(0, 2, 4, 2)
                store(0, 4, "scalar")
            turn_values(m + 1)
            if i == 2:
                product(0, 1, 0, 4)
                store(0, 0, "scalar")
                distances(3, 1)
            elif i == 3:
                product(1, 1, 0, 4)
                store(1, 0, "scalar")
            elif i == 4:
                product(2, 1, 0, 4)
                store(2, 0, "scalar")
                product(2, 1, 4, 4)
                store(2, 4, "scalar")
                product(0, 2, 8, 2)
            invert_total(i - 1)
            if i < QUERY_TILES:
                quantise_values(m - 2)
            normalise(i - 1, 0)
            normalise(i - 1, 1)
            turn_affinity(i - 1, 0)
            turn_affinity(i - 1, 1)
            if i == QUERY_TILES:
                store(0, 8, "scalar")
                quantise_values(m - 2)
            maximum(i)
            exponentials(i)
            if i == 0:
                query_norms(1, QUERY_TILES)
            if i != 2:
                distances(i + 1, 1)
            if i == 3:
                product(0, 2, 6, 2)
            turn_values(m + 2)
            distances(i + 1, 2)
            distances(i + 1, 3)
            if i != 3:
                quantise_values(m - 1)
            if i == 4:
                product(0, 2, 10, 2)
                store(0, 10, "scalar")
                product(2, 1, 8, 2)
                store(2, 8, "scalar")
            quantise_affinity(i - 1, 0)
            quantise_affinity(i - 1, 1)
            if i == 3:
                quantise_values(m - 1)
            quantise_values(m)
            if i == 3:
                store(0, 6, "vector")
        product(3, 1, 0, 4)
        store(3, 0, "scalar")
        product(3, 1, 4, 4)
        store(3, 4, "vector")
        product(3, 1, 8, 2)
        store(3, 8, "scalar")
        product(2, 2, 10, 1)
        store(2, 10, "vector")
        product(2, 1, 11, 1)
        store(2, 11, "scalar")
        product(3, 1, 11, 1)
        store(3, 11, "vector")
